import numpy as np
import ml_dtypes


def mxq(x, axis, fmt="e4m3"):
    dtype, down = {"e4m3": (ml_dtypes.float8_e4m3fn, 7), "e5m2": (ml_dtypes.float8_e5m2, 14)}[fmt]
    v = np.moveaxis(np.asarray(x, np.float32).astype(ml_dtypes.bfloat16).astype(np.float64), axis, -1)
    blocks = v.reshape(v.shape[:-1] + (-1, 32))
    amax = np.abs(blocks).max(-1, keepdims=True)
    byte = np.maximum(np.where(amax > 0, np.frexp(amax)[1] - 1 + 127, 0) - down, 1)
    scale = np.exp2(byte - 127.0)
    codes = (blocks / scale).astype(np.float32).astype(dtype).astype(np.float64)
    return np.moveaxis((codes * scale).reshape(v.shape), -1, axis)


WIDE = False


def mx_kscale(k):
    if not WIDE:
        return np.ones(k)
    levels = np.array([10, -10, 5, -5, 0])
    if k % 512:
        return np.exp2(np.random.permutation(np.resize(levels, k // 32))).repeat(32)
    a = np.empty((k // 512, 16))
    for p in range(k // 512):
        a[p, :8] = np.random.permutation(np.resize(levels, 8))
        for g in range(8):
            far = levels[np.abs(levels - a[p, g]) >= 10]
            a[p, g + 8] = far[np.random.randint(len(far))]
    return np.exp2(a.ravel()).repeat(32)


BF16 = ml_dtypes.bfloat16


def bf(x):
    return np.asarray(x, np.float32).astype(BF16)


def f64(x):
    return np.asarray(x).astype(np.float64)


B, S, D, H, HD, M, G = 4, 1024, 512, 4, 128, 512, 3
EPS = 1e-6
HH = H * HD


def silu(v):
    return v / (1.0 + np.exp(-v))


def rmsnorm(x, gain):
    var = np.mean(np.square(x), axis=-1, keepdims=True)
    return x * (1.0 / np.sqrt(var + EPS)) * gain


def setup_inputs():
    s, t = mx_kscale(HH), mx_kscale(D)
    return {"attn": bf(0.3 * np.random.standard_normal((B, S, HH)) * s),
            "x": bf(np.random.standard_normal((B, S, D))),
            "w_o": bf(np.random.standard_normal((HH, D)) * 2.0 / np.sqrt(HH) / s[:, None]),
            "rms2_scale": bf((1.0 + 0.1 * np.random.standard_normal(D)) * t),
            "w_gate": bf(np.random.standard_normal((D, M)) / np.sqrt(D) / t[:, None]),
            "w_up": bf(np.random.standard_normal((D, M)) / np.sqrt(D) / t[:, None])}


def reference(attn, x, w_o, rms2_scale, w_gate, w_up):
    x_mid = f64(x) + (mxq(f64(attn), 2, "e4m3") @ mxq(f64(w_o), 0, "e4m3"))
    hq = mxq(rmsnorm(x_mid, f64(rms2_scale)), 2, "e4m3")
    g = silu(hq @ mxq(f64(w_gate), 0, "e4m3")) * (hq @ mxq(f64(w_up), 0, "e4m3"))
    return x_mid, g

@@ -1,0 +1,249 @@
+from contextlib import ExitStack
+
+import concourse.mybir as mybir
+from concourse.masks import make_identity
+
+F32 = mybir.dt.float32
+BF16 = mybir.dt.bfloat16
+U32 = mybir.dt.uint32
+U8 = mybir.dt.uint8
+FP8X4 = mybir.dt.float8_e4m3fn_x4
+ALU = mybir.AluOpType
+ACT = mybir.ActivationFunctionType
+
+P = 128
+PACK = 4
+HALVES = 2
+D = 512
+TOKENS = 4096
+BLOCK = 2
+BLOCKS = TOKENS // (P * BLOCK)
+EPS = 1e-6
+
+FLOPS = 3 * 2 * TOKENS * D * D
+
+
+def tile_transformerblocktpu_pb_t_kernel(
+    tc, attn, x, w_o, rms2_scale, w_gate, w_up, out_0, out_1
+):
+    nc = tc.nc
+    attn_tiles = attn.flatten_outer_dims().rearrange("(p j) k -> p j k", p=P)
+    x_tiles = x.flatten_outer_dims().rearrange("(p j) k -> p j k", p=P)
+    x_mid_tiles = out_0.flatten_outer_dims().rearrange("(p j) k -> p j k", p=P)
+    g_tiles = out_1.flatten_outer_dims().rearrange("(p j) k -> p j k", p=P)
+
+    with ExitStack() as pools:
+        pools.enter_context(tc.manual_schedule())
+        keep = pools.enter_context(tc.tile_pool(name="keep", bufs=1))
+        stage = pools.enter_context(tc.tile_pool(name="stage", bufs=3))
+        loads = pools.enter_context(tc.tile_pool(name="loads", bufs=BLOCKS))
+        results = pools.enter_context(tc.tile_pool(name="results", bufs=4))
+        work = pools.enter_context(tc.tile_pool(name="work", bufs=3))
+        per_tile = pools.enter_context(tc.tile_pool(name="per_tile", bufs=3 * BLOCK))
+        word_banks = pools.enter_context(tc.psum_pool(name="word_banks", bufs=2))
+        product_banks = pools.enter_context(tc.psum_pool(name="product_banks", bufs=3 * BLOCK))
+
+        attn_in, x_in = {}, {}
+        attn_words, attn_grouped, attn_mx, attn_wo = {}, {}, {}, {}
+        x_mid, sum_sq, inv_rms, h = {}, {}, {}, {}
+        h_words, h_grouped, h_mx, gate_up, silu_gate = {}, {}, {}, {}, {}
+
+        def tiles_of(q):
+            return slice(q * BLOCK, (q + 1) * BLOCK)
+
+        def load_attn(q):
+            attn_in[q] = loads.tile([P, BLOCK, D], BF16, name="attn_in")
+            nc.sync.dma_start(out=attn_in[q][:], in_=attn_tiles[:, tiles_of(q), :])
+
+        def load_x(q):
+            x_in[q] = loads.tile([P, BLOCK, D], BF16, name="x_in")
+            nc.sync.dma_start(out=x_in[q][:], in_=x_tiles[:, tiles_of(q), :])
+
+        def load_weight(w):
+            raw = stage.tile([P, PACK, D], BF16)
+            nc.sync.dma_start(out=raw[:], in_=w.rearrange("(p t) n -> p t n", t=PACK))
+            return raw
+
+        def regroup_weight(raw, copy):
+            grouped = stage.tile([P, D, PACK], BF16, align_bytes=64)
+            copy(
+                out=grouped[:].rearrange("p (c i) t -> p c t i", i=4),
+                in_=raw[:].rearrange("p t (c i) -> p c t i", i=4),
+            )
+            return grouped
+
+        def quantise_weight(grouped, label):
+            codes = keep.tile([P, D], U32, name=label + "_codes", align_bytes=64)
+            scales = keep.tile([P, D], U8, name=label + "_scales", align_bytes=64)
+            nc.vector.quantize_mx(
+                out=codes[:].bitcast(FP8X4), scales=scales[:], in_=grouped[:].rearrange("p n t -> p (n t)")
+            )
+            return codes, scales
+
+        def transpose(rows):
+            words = word_banks.tile([P, BLOCK, HALVES, P], F32)
+            for b in range(BLOCK):
+                row_words = rows[:, b, :].bitcast(F32)
+                for u in range(HALVES):
+                    nc.tensor.transpose(words[:, b, u, :], row_words[:, u : HALVES * P : HALVES], identity[:])
+            return words
+
+        def regroup(words, label):
+            grouped = work.tile([P, BLOCK, P, PACK], BF16, tag=label + "_grouped", align_bytes=64)
+            nc.scalar.copy(out=grouped[:].bitcast(F32), in_=words[:].rearrange("p b u r -> p b r u"))
+            return grouped
+
+        def quantise(grouped, label):
+            codes = work.tile([P, BLOCK * P], U32, tag=label + "_codes", align_bytes=64)
+            scales = work.tile([P, BLOCK * P], U8, tag=label + "_scales", align_bytes=64)
+            nc.vector.quantize_mx(
+                out=codes[:].bitcast(FP8X4), scales=scales[:], in_=grouped[:].rearrange("p b r t -> p (b r t)")
+            )
+            return codes, scales
+
+        def product(rows_mx, b, weight_mx):
+            bank = product_banks.tile([P, D], F32)
+            tokens = slice(b * P, (b + 1) * P)
+            nc.tensor.matmul_mx(
+                out=bank[:],
+                lhsT=rows_mx[0][:, tokens].bitcast(FP8X4),
+                lhsT_scale=rows_mx[1][:, tokens],
+                rhs=weight_mx[0][:].bitcast(FP8X4),
+                rhs_scale=weight_mx[1][:],
+                start=True,
+                stop=True,
+            )
+            return bank
+
+        def transpose_attn(q):
+            attn_words[q] = transpose(attn_in[q])
+
+        def regroup_attn(q):
+            attn_grouped[q] = regroup(attn_words[q], "attn")
+
+        def quantise_attn(q):
+            attn_mx[q] = quantise(attn_grouped[q], "attn")
+
+        def multiply_by_w_o(q):
+            attn_wo[q] = [product(attn_mx[q], b, wo_mx) for b in range(BLOCK)]
+
+        def add_residual(q):
+            x_mid[q] = results.tile([P, BLOCK, D], F32, name="x_mid")
+            for b in range(BLOCK):
+                nc.vector.tensor_tensor(
+                    out=x_mid[q][:, b, :], in0=attn_wo[q][b][:], in1=x_in[q][:, b, :], op=ALU.add
+                )
+            nc.sync.dma_start(out=x_mid_tiles[:, tiles_of(q), :], in_=x_mid[q][:])
+
+        def sum_squares(q):
+            sum_sq[q] = work.tile([P, BLOCK], F32, name="sum_sq")
+            for b in range(BLOCK):
+                squares = per_tile.tile([P, D], BF16)
+                nc.scalar.activation(
+                    out=squares[:], in_=x_mid[q][:, b, :], func=ACT.Square, accum_out=sum_sq[q][:, b : b + 1]
+                )
+
+        def invert_rms(q):
+            mean_sq = work.tile([P, BLOCK], F32)
+            nc.gpsimd.tensor_scalar(
+                out=mean_sq[:], in0=sum_sq[q][:], scalar1=1.0 / D, scalar2=EPS, op0=ALU.mult, op1=ALU.add
+            )
+            inv_rms[q] = work.tile([P, BLOCK], F32, name="inv_rms")
+            nc.gpsimd.tensor_tensor(out=inv_rms[q][:], in0=mean_sq[:], in1=minus_half[:], op=ALU.pow)
+
+        def normalise(q):
+            h[q] = work.tile([P, BLOCK, D], BF16, name="h")
+            for b in range(BLOCK):
+                nc.vector.scalar_tensor_tensor(
+                    out=h[q][:, b, :],
+                    in0=x_mid[q][:, b, :],
+                    scalar=inv_rms[q][:, b : b + 1],
+                    in1=gain[:],
+                    op0=ALU.mult,
+                    op1=ALU.mult,
+                )
+
+        def transpose_h(q):
+            h_words[q] = transpose(h[q])
+
+        def regroup_h(q):
+            h_grouped[q] = regroup(h_words[q], "h")
+
+        def quantise_h(q):
+            h_mx[q] = quantise(h_grouped[q], "h")
+
+        def multiply_by_gate_and_up(q):
+            gate_up[q] = [
+                (product(h_mx[q], b, wg_mx), product(h_mx[q], b, wu_mx)) for b in range(BLOCK)
+            ]
+
+        def apply_silu(q):
+            silu_gate[q] = []
+            for b in range(BLOCK):
+                silu_b = per_tile.tile([P, D], F32)
+                nc.scalar.activation(out=silu_b[:], in_=gate_up[q][b][0][:], func=ACT.Silu)
+                silu_gate[q].append(silu_b)
+
+        def multiply_gate_and_up(q):
+            for b in range(BLOCK):
+                g = per_tile.tile([P, D], F32)
+                nc.vector.tensor_tensor(out=g[:], in0=gate_up[q][b][1][:], in1=silu_gate[q][b][:], op=ALU.mult)
+                nc.sync.dma_start(out=g_tiles[:, q * BLOCK + b, :], in_=g[:])
+
+        identity = keep.tile([P, P], F32)
+        make_identity(nc, identity[:])
+        gain_row = keep.tile([P, D], BF16)
+        nc.vector.memset(gain_row[:], 0.0)
+        ones = keep.tile([P, P], BF16)
+        nc.vector.memset(ones[:], 1.0)
+        minus_half = keep.tile([P, BLOCK], F32)
+        nc.vector.memset(minus_half[:], -0.5)
+
+        table_warmer = keep.tile([P, BLOCK], F32)
+        nc.scalar.activation(out=table_warmer[:], in_=minus_half[:], func=ACT.Silu)
+
+        wo_raw = load_weight(w_o)
+        nc.sync.dma_start(out=gain_row[0:1, :], in_=rms2_scale.rearrange("(o n) -> o n", o=1))
+        load_attn(0)
+        load_x(0)
+        load_attn(1)
+        load_attn(2)
+        wg_raw = load_weight(w_gate)
+        wu_raw = load_weight(w_up)
+        load_x(1)
+        load_attn(3)
+        load_x(2)
+
+        gain_bank = product_banks.tile([P, D], F32, tag="bank")
+        nc.tensor.matmul(out=gain_bank[:], lhsT=ones[:], rhs=gain_row[:], start=True, stop=True)
+        gain = keep.tile([P, D], F32)
+        nc.scalar.copy(out=gain[:], in_=gain_bank[:])
+        wo_mx = quantise_weight(regroup_weight(wo_raw, nc.vector.tensor_copy), "wo")
+
+        def at(q, stage_of_block):
+            if 0 <= q < BLOCKS:
+                stage_of_block(q)
+
+        for step in range(-2, BLOCKS + 4):
+            at(step + 6, load_attn)
+            at(step + 5, load_x)
+            at(step - 2, transpose_h)
+            at(step + 2, transpose_attn)
+            at(step + 1, quantise_attn)
+            at(step - 3, quantise_h)
+            at(step - 4, apply_silu)
+            at(step - 2, regroup_h)
+            at(step + 2, regroup_attn)
+            at(step, add_residual)
+            at(step + 1, multiply_by_w_o)
+            at(step - 4, multiply_gate_and_up)
+            at(step - 3, multiply_by_gate_and_up)
+            at(step, sum_squares)
+            at(step, invert_rms)
+            at(step - 1, normalise)
+            if step == 0:
+                wg_grouped = regroup_weight(wg_raw, nc.vector.tensor_copy)
+                wu_grouped = regroup_weight(wu_raw, nc.scalar.copy)
+            if step == 1:
+                wg_mx = quantise_weight(wg_grouped, "wg")
+                wu_mx = quantise_weight(wu_grouped, "wu")

@@ -45,7 +45,7 @@ def tile_transformerblocktpu_pb_t_kernel(
 
         attn_in, x_in = {}, {}
         attn_words, attn_grouped, attn_mx, attn_wo = {}, {}, {}, {}
-        x_mid, sum_sq, inv_rms, h = {}, {}, {}, {}
+        x_mid, sum_sq, mean_sq, inv_rms, h = {}, {}, {}, {}, {}
         h_words, h_grouped, h_mx, gate_up, silu_gate = {}, {}, {}, {}, {}
 
         def tiles_of(q):
@@ -143,13 +143,15 @@ def tile_transformerblocktpu_pb_t_kernel(
                     out=squares[:], in_=x_mid[q][:, b, :], func=ACT.Square, accum_out=sum_sq[q][:, b : b + 1]
                 )
 
-        def invert_rms(q):
-            mean_sq = work.tile([P, BLOCK], F32)
-            nc.gpsimd.tensor_scalar(
-                out=mean_sq[:], in0=sum_sq[q][:], scalar1=1.0 / D, scalar2=EPS, op0=ALU.mult, op1=ALU.add
+        def mean_squares(q):
+            mean_sq[q] = work.tile([P, BLOCK], F32, name="mean_sq")
+            nc.vector.tensor_scalar(
+                out=mean_sq[q][:], in0=sum_sq[q][:], scalar1=1.0 / D, scalar2=EPS, op0=ALU.mult, op1=ALU.add
             )
+
+        def invert_rms(q):
             inv_rms[q] = work.tile([P, BLOCK], F32, name="inv_rms")
-            nc.gpsimd.tensor_tensor(out=inv_rms[q][:], in0=mean_sq[:], in1=minus_half[:], op=ALU.pow)
+            nc.gpsimd.tensor_tensor(out=inv_rms[q][:], in0=mean_sq[q][:], in1=minus_half[:], op=ALU.pow)
 
         def normalise(q):
             h[q] = work.tile([P, BLOCK, D], BF16, name="h")
@@ -231,6 +233,8 @@ def tile_transformerblocktpu_pb_t_kernel(
             at(step + 2, transpose_attn)
             at(step + 1, quantise_attn)
             at(step - 3, quantise_h)
+            at(step - 1, mean_squares)
+            at(step - 1, invert_rms)
             at(step - 4, apply_silu)
             at(step - 2, regroup_h)
             at(step + 2, regroup_attn)
@@ -239,7 +243,6 @@ def tile_transformerblocktpu_pb_t_kernel(
             at(step - 4, multiply_gate_and_up)
             at(step - 3, multiply_by_gate_and_up)
             at(step, sum_squares)
-            at(step, invert_rms)
             at(step - 1, normalise)
             if step == 0:
                 wg_grouped = regroup_weight(wg_raw, nc.vector.tensor_copy)

@@ -19,6 +19,7 @@ TOKENS = 4096
 BLOCK = 2
 BLOCKS = TOKENS // (P * BLOCK)
 EPS = 1e-6
+SHARED = 256
 
 FLOPS = 3 * 2 * TOKENS * D * D
 
@@ -45,7 +46,7 @@ def tile_transformerblocktpu_pb_t_kernel(
 
         attn_in, x_in = {}, {}
         attn_words, attn_grouped, attn_mx, attn_wo = {}, {}, {}, {}
-        x_mid, sum_sq, mean_sq, inv_rms, h = {}, {}, {}, {}, {}
+        x_mid, sum_sq, mean_sq, inv_rms, scaled, h = {}, {}, {}, {}, {}, {}
         h_words, h_grouped, h_mx, gate_up, silu_gate = {}, {}, {}, {}, {}
 
         def tiles_of(q):
@@ -153,14 +154,25 @@ def tile_transformerblocktpu_pb_t_kernel(
             inv_rms[q] = work.tile([P, BLOCK], F32, name="inv_rms")
             nc.gpsimd.tensor_tensor(out=inv_rms[q][:], in0=mean_sq[q][:], in1=minus_half[:], op=ALU.pow)
 
-        def normalise(q):
+        def scale_by_gain(q):
+            scaled[q] = work.tile([P, SHARED], F32, name="scaled")
+            nc.gpsimd.tensor_tensor(
+                out=scaled[q][:], in0=x_mid[q][:, 0, :SHARED], in1=gain[:, :SHARED], op=ALU.mult
+            )
+
+        def scale_by_inv_rms(q):
             h[q] = work.tile([P, BLOCK, D], BF16, name="h")
-            for b in range(BLOCK):
+            nc.scalar.activation(
+                out=h[q][:, 0, :SHARED], in_=scaled[q][:], func=ACT.Copy, scale=inv_rms[q][:, 0:1]
+            )
+
+        def normalise(q):
+            for b, first in ((0, SHARED), (1, 0)):
                 nc.vector.scalar_tensor_tensor(
-                    out=h[q][:, b, :],
-                    in0=x_mid[q][:, b, :],
+                    out=h[q][:, b, first:],
+                    in0=x_mid[q][:, b, first:],
                     scalar=inv_rms[q][:, b : b + 1],
-                    in1=gain[:],
+                    in1=gain[:, first:],
                     op0=ALU.mult,
                     op1=ALU.mult,
                 )
@@ -242,7 +254,9 @@ def tile_transformerblocktpu_pb_t_kernel(
             at(step + 1, multiply_by_w_o)
             at(step - 4, multiply_gate_and_up)
             at(step - 3, multiply_by_gate_and_up)
+            at(step - 1, scale_by_inv_rms)
             at(step, sum_squares)
+            at(step, scale_by_gain)
             at(step - 1, normalise)
             if step == 0:
                 wg_grouped = regroup_weight(wg_raw, nc.vector.tensor_copy)

@@ -47,7 +47,7 @@ def tile_transformerblocktpu_pb_t_kernel(
         attn_in, x_in = {}, {}
         attn_words, attn_grouped, attn_mx, attn_wo = {}, {}, {}, {}
         x_mid, sum_sq, mean_sq, inv_rms, scaled, h = {}, {}, {}, {}, {}, {}
-        h_words, h_grouped, h_mx, gate_up, silu_gate = {}, {}, {}, {}, {}
+        h_words, h_grouped, h_mx, gate, up, silu_gate = {}, {}, {}, {}, {}, {}
 
         def tiles_of(q):
             return slice(q * BLOCK, (q + 1) * BLOCK)
@@ -125,24 +125,25 @@ def tile_transformerblocktpu_pb_t_kernel(
         def quantise_attn(q):
             attn_mx[q] = quantise(attn_grouped[q], "attn")
 
-        def multiply_by_w_o(q):
-            attn_wo[q] = [product(attn_mx[q], b, wo_mx) for b in range(BLOCK)]
+        def multiply_by_w_o(q, b):
+            attn_wo[q, b] = product(attn_mx[q], b, wo_mx)
 
-        def add_residual(q):
-            x_mid[q] = results.tile([P, BLOCK, D], F32, name="x_mid")
-            for b in range(BLOCK):
-                nc.vector.tensor_tensor(
-                    out=x_mid[q][:, b, :], in0=attn_wo[q][b][:], in1=x_in[q][:, b, :], op=ALU.add
-                )
-            nc.sync.dma_start(out=x_mid_tiles[:, tiles_of(q), :], in_=x_mid[q][:])
+        def add_residual(q, b):
+            if b == 0:
+                x_mid[q] = results.tile([P, BLOCK, D], F32, name="x_mid")
+            nc.vector.tensor_tensor(
+                out=x_mid[q][:, b, :], in0=attn_wo[q, b][:], in1=x_in[q][:, b, :], op=ALU.add
+            )
+            if b == BLOCK - 1:
+                nc.sync.dma_start(out=x_mid_tiles[:, tiles_of(q), :], in_=x_mid[q][:])
 
-        def sum_squares(q):
-            sum_sq[q] = work.tile([P, BLOCK], F32, name="sum_sq")
-            for b in range(BLOCK):
-                squares = per_tile.tile([P, D], BF16)
-                nc.scalar.activation(
-                    out=squares[:], in_=x_mid[q][:, b, :], func=ACT.Square, accum_out=sum_sq[q][:, b : b + 1]
-                )
+        def sum_squares(q, b):
+            if b == 0:
+                sum_sq[q] = work.tile([P, BLOCK], F32, name="sum_sq")
+            squares = per_tile.tile([P, D], BF16)
+            nc.scalar.activation(
+                out=squares[:], in_=x_mid[q][:, b, :], func=ACT.Square, accum_out=sum_sq[q][:, b : b + 1]
+            )
 
         def mean_squares(q):
             mean_sq[q] = work.tile([P, BLOCK], F32, name="mean_sq")
@@ -166,16 +167,16 @@ def tile_transformerblocktpu_pb_t_kernel(
                 out=h[q][:, 0, :SHARED], in_=scaled[q][:], func=ACT.Copy, scale=inv_rms[q][:, 0:1]
             )
 
-        def normalise(q):
-            for b, first in ((0, SHARED), (1, 0)):
-                nc.vector.scalar_tensor_tensor(
-                    out=h[q][:, b, first:],
-                    in0=x_mid[q][:, b, first:],
-                    scalar=inv_rms[q][:, b : b + 1],
-                    in1=gain[:, first:],
-                    op0=ALU.mult,
-                    op1=ALU.mult,
-                )
+        def normalise(q, b):
+            first = SHARED if b == 0 else 0
+            nc.vector.scalar_tensor_tensor(
+                out=h[q][:, b, first:],
+                in0=x_mid[q][:, b, first:],
+                scalar=inv_rms[q][:, b : b + 1],
+                in1=gain[:, first:],
+                op0=ALU.mult,
+                op1=ALU.mult,
+            )
 
         def transpose_h(q):
             h_words[q] = transpose(h[q])
@@ -186,23 +187,20 @@ def tile_transformerblocktpu_pb_t_kernel(
         def quantise_h(q):
             h_mx[q] = quantise(h_grouped[q], "h")
 
-        def multiply_by_gate_and_up(q):
-            gate_up[q] = [
-                (product(h_mx[q], b, wg_mx), product(h_mx[q], b, wu_mx)) for b in range(BLOCK)
-            ]
+        def multiply_by_w_gate(q, b):
+            gate[q, b] = product(h_mx[q], b, wg_mx)
 
-        def apply_silu(q):
-            silu_gate[q] = []
-            for b in range(BLOCK):
-                silu_b = per_tile.tile([P, D], F32)
-                nc.scalar.activation(out=silu_b[:], in_=gate_up[q][b][0][:], func=ACT.Silu)
-                silu_gate[q].append(silu_b)
+        def multiply_by_w_up(q, b):
+            up[q, b] = product(h_mx[q], b, wu_mx)
 
-        def multiply_gate_and_up(q):
-            for b in range(BLOCK):
-                g = per_tile.tile([P, D], F32)
-                nc.vector.tensor_tensor(out=g[:], in0=gate_up[q][b][1][:], in1=silu_gate[q][b][:], op=ALU.mult)
-                nc.sync.dma_start(out=g_tiles[:, q * BLOCK + b, :], in_=g[:])
+        def apply_silu(q, b):
+            silu_gate[q, b] = per_tile.tile([P, D], F32, name="silu_gate")
+            nc.scalar.activation(out=silu_gate[q, b][:], in_=gate[q, b][:], func=ACT.Silu)
+
+        def multiply_gate_and_up(q, b):
+            g = per_tile.tile([P, D], F32)
+            nc.vector.tensor_tensor(out=g[:], in0=up[q, b][:], in1=silu_gate[q, b][:], op=ALU.mult)
+            nc.sync.dma_start(out=g_tiles[:, q * BLOCK + b, :], in_=g[:])
 
         identity = keep.tile([P, P], F32)
         make_identity(nc, identity[:])
@@ -234,9 +232,9 @@ def tile_transformerblocktpu_pb_t_kernel(
         nc.scalar.copy(out=gain[:], in_=gain_bank[:])
         wo_mx = quantise_weight(regroup_weight(wo_raw, nc.vector.tensor_copy), "wo")
 
-        def at(q, stage_of_block):
+        def at(q, stage_of_block, *tile):
             if 0 <= q < BLOCKS:
-                stage_of_block(q)
+                stage_of_block(q, *tile)
 
         for step in range(-2, BLOCKS + 4):
             at(step + 6, load_attn)
@@ -247,20 +245,31 @@ def tile_transformerblocktpu_pb_t_kernel(
             at(step - 3, quantise_h)
             at(step - 1, mean_squares)
             at(step - 1, invert_rms)
-            at(step - 4, apply_silu)
+            at(step - 4, apply_silu, 0)
+            at(step - 4, apply_silu, 1)
             at(step - 2, regroup_h)
             at(step + 2, regroup_attn)
-            at(step, add_residual)
-            at(step + 1, multiply_by_w_o)
-            at(step - 4, multiply_gate_and_up)
-            at(step - 3, multiply_by_gate_and_up)
+            at(step - 3, multiply_by_w_gate, 0)
+            at(step - 3, multiply_by_w_gate, 1)
+            at(step, add_residual, 0)
+            at(step, add_residual, 1)
+            at(step + 1, multiply_by_w_o, 0)
+            at(step + 1, multiply_by_w_o, 1)
+            at(step - 4, multiply_gate_and_up, 0)
+            at(step - 4, multiply_gate_and_up, 1)
+            at(step - 3, multiply_by_w_up, 0)
+            at(step - 3, multiply_by_w_up, 1)
             at(step - 1, scale_by_inv_rms)
-            at(step, sum_squares)
+            at(step, sum_squares, 0)
+            at(step, sum_squares, 1)
             at(step, scale_by_gain)
-            at(step - 1, normalise)
+            at(step - 1, normalise, 0)
+            at(step - 1, normalise, 1)
             if step == 0:
                 wg_grouped = regroup_weight(wg_raw, nc.vector.tensor_copy)
+            if step == 0:
                 wu_grouped = regroup_weight(wu_raw, nc.scalar.copy)
             if step == 1:
                 wg_mx = quantise_weight(wg_grouped, "wg")
+            if step == 1:
                 wu_mx = quantise_weight(wu_grouped, "wu")

@@ -19,6 +19,7 @@ TOKENS = 4096
 BLOCK = 2
 BLOCKS = TOKENS // (P * BLOCK)
 EPS = 1e-6
+FIRST_SHARED = 4
 SHARED = 256
 
 FLOPS = 3 * 2 * TOKENS * D * D
@@ -156,6 +157,8 @@ def tile_transformerblocktpu_pb_t_kernel(
             nc.gpsimd.tensor_tensor(out=inv_rms[q][:], in0=mean_sq[q][:], in1=minus_half[:], op=ALU.pow)
 
         def scale_by_gain(q):
+            if q < FIRST_SHARED:
+                return
             scaled[q] = work.tile([P, SHARED], F32, name="scaled")
             nc.gpsimd.tensor_tensor(
                 out=scaled[q][:], in0=x_mid[q][:, 0, :SHARED], in1=gain[:, :SHARED], op=ALU.mult
@@ -163,12 +166,14 @@ def tile_transformerblocktpu_pb_t_kernel(
 
         def scale_by_inv_rms(q):
             h[q] = work.tile([P, BLOCK, D], BF16, name="h")
+            if q < FIRST_SHARED:
+                return
             nc.scalar.activation(
                 out=h[q][:, 0, :SHARED], in_=scaled[q][:], func=ACT.Copy, scale=inv_rms[q][:, 0:1]
             )
 
         def normalise(q, b):
-            first = SHARED if b == 0 else 0
+            first = SHARED if b == 0 and q >= FIRST_SHARED else 0
             nc.vector.scalar_tensor_tensor(
                 out=h[q][:, b, first:],
                 in0=x_mid[q][:, b, first:],
@@ -202,8 +207,15 @@ def tile_transformerblocktpu_pb_t_kernel(
             nc.vector.tensor_tensor(out=g[:], in0=up[q, b][:], in1=silu_gate[q, b][:], op=ALU.mult)
             nc.sync.dma_start(out=g_tiles[:, q * BLOCK + b, :], in_=g[:])
 
+        def keep_warm(products):
+            bank = product_banks.tile([P, D], F32)
+            for i in range(products):
+                nc.tensor.matmul(out=bank[:], lhsT=zeros[:, :P], rhs=zeros[:], start=True, stop=True)
+
         identity = keep.tile([P, P], F32)
         make_identity(nc, identity[:])
+        zeros = keep.tile([P, D], BF16)
+        nc.vector.memset(zeros[:], 0.0)
         gain_row = keep.tile([P, D], BF16)
         nc.vector.memset(gain_row[:], 0.0)
         ones = keep.tile([P, P], BF16)
@@ -215,40 +227,124 @@ def tile_transformerblocktpu_pb_t_kernel(
         nc.scalar.activation(out=table_warmer[:], in_=minus_half[:], func=ACT.Silu)
 
         wo_raw = load_weight(w_o)
-        nc.sync.dma_start(out=gain_row[0:1, :], in_=rms2_scale.rearrange("(o n) -> o n", o=1))
         load_attn(0)
-        load_x(0)
         load_attn(1)
+        nc.sync.dma_start(out=gain_row[0:1, :], in_=rms2_scale.rearrange("(o n) -> o n", o=1))
+        load_x(0)
+        wu_raw = load_weight(w_up)
         load_attn(2)
         wg_raw = load_weight(w_gate)
-        wu_raw = load_weight(w_up)
         load_x(1)
         load_attn(3)
         load_x(2)
-
-        gain_bank = product_banks.tile([P, D], F32, tag="bank")
-        nc.tensor.matmul(out=gain_bank[:], lhsT=ones[:], rhs=gain_row[:], start=True, stop=True)
-        gain = keep.tile([P, D], F32)
-        nc.scalar.copy(out=gain[:], in_=gain_bank[:])
-        wo_mx = quantise_weight(regroup_weight(wo_raw, nc.vector.tensor_copy), "wo")
+        load_attn(4)
+        load_x(3)
+        load_attn(5)
+        load_x(4)
+        load_attn(6)
+        load_x(5)
+        load_attn(7)
+        load_x(6)
+        load_attn(8)
+        load_x(7)
+        load_attn(9)
+        load_x(8)
 
         def at(q, stage_of_block, *tile):
             if 0 <= q < BLOCKS:
                 stage_of_block(q, *tile)
 
-        for step in range(-2, BLOCKS + 4):
+        keep_warm(5)
+        transpose_attn(0)
+        wo_grouped = regroup_weight(wo_raw, nc.vector.tensor_copy)
+        regroup_attn(0)
+        wo_mx = quantise_weight(wo_grouped, "wo")
+        quantise_attn(0)
+        transpose_attn(1)
+        multiply_by_w_o(0, 0)
+        multiply_by_w_o(0, 1)
+        gain_bank = product_banks.tile([P, D], F32, tag="bank")
+        nc.tensor.matmul(out=gain_bank[:], lhsT=ones[:], rhs=gain_row[:], start=True, stop=True)
+        regroup_attn(1)
+        wu_grouped = regroup_weight(wu_raw, nc.scalar.copy)
+        add_residual(0, 0)
+        add_residual(0, 1)
+        quantise_attn(1)
+        wg_grouped = regroup_weight(wg_raw, nc.vector.tensor_copy)
+        transpose_attn(2)
+        multiply_by_w_o(1, 0)
+        multiply_by_w_o(1, 1)
+        sum_squares(0, 0)
+        sum_squares(0, 1)
+        regroup_attn(2)
+        gain = keep.tile([P, D], F32)
+        nc.scalar.copy(out=gain[:], in_=gain_bank[:])
+        add_residual(1, 0)
+        mean_squares(0)
+        invert_rms(0)
+        add_residual(1, 1)
+        quantise_attn(2)
+        wg_mx = quantise_weight(wg_grouped, "wg")
+        transpose_attn(3)
+        multiply_by_w_o(2, 0)
+        multiply_by_w_o(2, 1)
+        scale_by_inv_rms(0)
+        sum_squares(1, 0)
+        sum_squares(1, 1)
+        regroup_attn(3)
+        normalise(0, 0)
+        normalise(0, 1)
+        transpose_attn(4)
+        transpose_h(0)
+        mean_squares(1)
+        invert_rms(1)
+        quantise_attn(3)
+        wu_mx = quantise_weight(wu_grouped, "wu")
+        regroup_attn(4)
+        regroup_h(0)
+        add_residual(2, 0)
+        add_residual(2, 1)
+        multiply_by_w_o(3, 0)
+        multiply_by_w_o(3, 1)
+        scale_by_inv_rms(1)
+        sum_squares(2, 0)
+        sum_squares(2, 1)
+        normalise(1, 0)
+        normalise(1, 1)
+        transpose_attn(5)
+        transpose_h(1)
+        mean_squares(2)
+        invert_rms(2)
+        quantise_attn(4)
+        quantise_h(0)
+        regroup_attn(5)
+        regroup_h(1)
+        multiply_by_w_gate(0, 0)
+        multiply_by_w_gate(0, 1)
+        add_residual(3, 0)
+        add_residual(3, 1)
+        multiply_by_w_o(4, 0)
+        multiply_by_w_o(4, 1)
+        multiply_by_w_up(0, 0)
+        multiply_by_w_up(0, 1)
+        scale_by_inv_rms(2)
+        sum_squares(3, 0)
+        sum_squares(3, 1)
+        normalise(2, 0)
+        normalise(2, 1)
+        for step in range(4, BLOCKS + 4):
             at(step + 6, load_attn)
             at(step + 5, load_x)
-            at(step - 2, transpose_h)
             at(step + 2, transpose_attn)
+            at(step - 2, transpose_h)
             at(step + 1, quantise_attn)
             at(step - 3, quantise_h)
             at(step - 1, mean_squares)
             at(step - 1, invert_rms)
             at(step - 4, apply_silu, 0)
             at(step - 4, apply_silu, 1)
-            at(step - 2, regroup_h)
             at(step + 2, regroup_attn)
+            at(step - 2, regroup_h)
             at(step - 3, multiply_by_w_gate, 0)
             at(step - 3, multiply_by_w_gate, 1)
             at(step, add_residual, 0)
@@ -265,11 +361,3 @@ def tile_transformerblocktpu_pb_t_kernel(
             at(step, scale_by_gain)
             at(step - 1, normalise, 0)
             at(step - 1, normalise, 1)
-            if step == 0:
-                wg_grouped = regroup_weight(wg_raw, nc.vector.tensor_copy)
-            if step == 0:
-                wu_grouped = regroup_weight(wu_raw, nc.scalar.copy)
-            if step == 1:
-                wg_mx = quantise_weight(wg_grouped, "wg")
-            if step == 1:
-                wu_mx = quantise_weight(wu_grouped, "wu")

@@ -20,7 +20,8 @@ BLOCK = 2
 BLOCKS = TOKENS // (P * BLOCK)
 EPS = 1e-6
 FIRST_SHARED = 4
-SHARED = 256
+SCALAR = 256
+SHARED = 384
 
 FLOPS = 3 * 2 * TOKENS * D * D
 
@@ -46,9 +47,9 @@ def tile_transformerblocktpu_pb_t_kernel(
         product_banks = pools.enter_context(tc.psum_pool(name="product_banks", bufs=3 * BLOCK))
 
         attn_in, x_in = {}, {}
-        attn_words, attn_grouped, attn_mx, attn_wo = {}, {}, {}, {}
+        grouped, attn_words, attn_mx, attn_wo = {}, {}, {}, {}
         x_mid, sum_sq, mean_sq, inv_rms, scaled, h = {}, {}, {}, {}, {}, {}
-        h_words, h_grouped, h_mx, gate, up, silu_gate = {}, {}, {}, {}, {}, {}
+        h_words, h_mx, gate, up, silu_gate = {}, {}, {}, {}, {}
 
         def tiles_of(q):
             return slice(q * BLOCK, (q + 1) * BLOCK)
@@ -90,18 +91,27 @@ def tile_transformerblocktpu_pb_t_kernel(
                     nc.tensor.transpose(words[:, b, u, :], row_words[:, u : HALVES * P : HALVES], identity[:])
             return words
 
-        def regroup(words, label):
-            grouped = work.tile([P, BLOCK, P, PACK], BF16, tag=label + "_grouped", align_bytes=64)
-            nc.scalar.copy(out=grouped[:].bitcast(F32), in_=words[:].rearrange("p b u r -> p b r u"))
-            return grouped
+        def regroup(step, place, words):
+            if step not in grouped:
+                grouped[step] = work.tile([P, 2, BLOCK, P, PACK], BF16, name="grouped", align_bytes=64), []
+            rows, places = grouped[step]
+            places.append(place)
+            nc.scalar.copy(out=rows[:, place, :, :, :].bitcast(F32), in_=words[:].rearrange("p b u r -> p b r u"))
 
-        def quantise(grouped, label):
-            codes = work.tile([P, BLOCK * P], U32, tag=label + "_codes", align_bytes=64)
-            scales = work.tile([P, BLOCK * P], U8, tag=label + "_scales", align_bytes=64)
+        def quantise(step):
+            if step not in grouped:
+                return
+            rows, places = grouped[step]
+            codes = work.tile([P, 2, BLOCK * P], U32, name="codes", align_bytes=64)
+            scales = work.tile([P, 2, BLOCK * P], U8, name="scales", align_bytes=64)
+            filled = slice(min(places), max(places) + 1)
             nc.vector.quantize_mx(
-                out=codes[:].bitcast(FP8X4), scales=scales[:], in_=grouped[:].rearrange("p b r t -> p (b r t)")
+                out=codes[:, filled, :].rearrange("p c r -> p (c r)").bitcast(FP8X4),
+                scales=scales[:, filled, :].rearrange("p c r -> p (c r)"),
+                in_=rows[:, filled, :, :, :].rearrange("p c b r t -> p (c b r t)"),
             )
-            return codes, scales
+            h_mx[step - 2] = codes[:, 0, :], scales[:, 0, :]
+            attn_mx[step + 2] = codes[:, 1, :], scales[:, 1, :]
 
         def product(rows_mx, b, weight_mx):
             bank = product_banks.tile([P, D], F32)
@@ -121,10 +131,7 @@ def tile_transformerblocktpu_pb_t_kernel(
             attn_words[q] = transpose(attn_in[q])
 
         def regroup_attn(q):
-            attn_grouped[q] = regroup(attn_words[q], "attn")
-
-        def quantise_attn(q):
-            attn_mx[q] = quantise(attn_grouped[q], "attn")
+            regroup(q - 2, 1, attn_words[q])
 
         def multiply_by_w_o(q, b):
             attn_wo[q, b] = product(attn_mx[q], b, wo_mx)
@@ -169,11 +176,17 @@ def tile_transformerblocktpu_pb_t_kernel(
             if q < FIRST_SHARED:
                 return
             nc.scalar.activation(
-                out=h[q][:, 0, :SHARED], in_=scaled[q][:], func=ACT.Copy, scale=inv_rms[q][:, 0:1]
+                out=h[q][:, 0, :SCALAR], in_=scaled[q][:, :SCALAR], func=ACT.Copy, scale=inv_rms[q][:, 0:1]
             )
 
         def normalise(q, b):
             first = SHARED if b == 0 and q >= FIRST_SHARED else 0
+            if first > 0 and SCALAR < SHARED:
+                nc.vector.tensor_scalar(
+                    out=h[q][:, 0, SCALAR:SHARED], in0=scaled[q][:, SCALAR:], scalar1=inv_rms[q][:, 0:1], scalar2=0.0, op0=ALU.mult, op1=ALU.add
+                )
+            if first == D:
+                return
             nc.vector.scalar_tensor_tensor(
                 out=h[q][:, b, first:],
                 in0=x_mid[q][:, b, first:],
@@ -187,10 +200,7 @@ def tile_transformerblocktpu_pb_t_kernel(
             h_words[q] = transpose(h[q])
 
         def regroup_h(q):
-            h_grouped[q] = regroup(h_words[q], "h")
-
-        def quantise_h(q):
-            h_mx[q] = quantise(h_grouped[q], "h")
+            regroup(q + 2, 0, h_words[q])
 
         def multiply_by_w_gate(q, b):
             gate[q, b] = product(h_mx[q], b, wg_mx)
@@ -259,7 +269,7 @@ def tile_transformerblocktpu_pb_t_kernel(
         wo_grouped = regroup_weight(wo_raw, nc.vector.tensor_copy)
         regroup_attn(0)
         wo_mx = quantise_weight(wo_grouped, "wo")
-        quantise_attn(0)
+        quantise(-2)
         transpose_attn(1)
         multiply_by_w_o(0, 0)
         multiply_by_w_o(0, 1)
@@ -269,7 +279,7 @@ def tile_transformerblocktpu_pb_t_kernel(
         wu_grouped = regroup_weight(wu_raw, nc.scalar.copy)
         add_residual(0, 0)
         add_residual(0, 1)
-        quantise_attn(1)
+        quantise(-1)
         wg_grouped = regroup_weight(wg_raw, nc.vector.tensor_copy)
         transpose_attn(2)
         multiply_by_w_o(1, 0)
@@ -283,7 +293,7 @@ def tile_transformerblocktpu_pb_t_kernel(
         mean_squares(0)
         invert_rms(0)
         add_residual(1, 1)
-        quantise_attn(2)
+        quantise(0)
         wg_mx = quantise_weight(wg_grouped, "wg")
         transpose_attn(3)
         multiply_by_w_o(2, 0)
@@ -298,7 +308,7 @@ def tile_transformerblocktpu_pb_t_kernel(
         transpose_h(0)
         mean_squares(1)
         invert_rms(1)
-        quantise_attn(3)
+        quantise(1)
         wu_mx = quantise_weight(wu_grouped, "wu")
         regroup_attn(4)
         regroup_h(0)
@@ -315,8 +325,7 @@ def tile_transformerblocktpu_pb_t_kernel(
         transpose_h(1)
         mean_squares(2)
         invert_rms(2)
-        quantise_attn(4)
-        quantise_h(0)
+        quantise(2)
         regroup_attn(5)
         regroup_h(1)
         multiply_by_w_gate(0, 0)
@@ -337,8 +346,7 @@ def tile_transformerblocktpu_pb_t_kernel(
             at(step + 5, load_x)
             at(step + 2, transpose_attn)
             at(step - 2, transpose_h)
-            at(step + 1, quantise_attn)
-            at(step - 3, quantise_h)
+            quantise(step - 1)
             at(step - 1, mean_squares)
             at(step - 1, invert_rms)
             at(step - 4, apply_silu, 0)

@@ -19,9 +19,15 @@ TOKENS = 4096
 BLOCK = 2
 BLOCKS = TOKENS // (P * BLOCK)
 EPS = 1e-6
-FIRST_SHARED = 4
-SCALAR = 256
-SHARED = 384
+
+ATTN_LEAD = 2
+H_LAG = 2
+G_LAG = 4
+
+GAIN_ON_GPSIMD = 384
+INV_ON_SCALAR = 256
+FIRST_SHARED = G_LAG
+WARM_PRODUCTS = 5
 
 FLOPS = 3 * 2 * TOKENS * D * D
 
@@ -38,7 +44,7 @@ def tile_transformerblocktpu_pb_t_kernel(
     with ExitStack() as pools:
         pools.enter_context(tc.manual_schedule())
         keep = pools.enter_context(tc.tile_pool(name="keep", bufs=1))
-        stage = pools.enter_context(tc.tile_pool(name="stage", bufs=3))
+        weights = pools.enter_context(tc.tile_pool(name="weights", bufs=3))
         loads = pools.enter_context(tc.tile_pool(name="loads", bufs=BLOCKS))
         results = pools.enter_context(tc.tile_pool(name="results", bufs=4))
         work = pools.enter_context(tc.tile_pool(name="work", bufs=3))
@@ -47,9 +53,9 @@ def tile_transformerblocktpu_pb_t_kernel(
         product_banks = pools.enter_context(tc.psum_pool(name="product_banks", bufs=3 * BLOCK))
 
         attn_in, x_in = {}, {}
-        grouped, attn_words, attn_mx, attn_wo = {}, {}, {}, {}
-        x_mid, sum_sq, mean_sq, inv_rms, scaled, h = {}, {}, {}, {}, {}, {}
-        h_words, h_mx, gate, up, silu_gate = {}, {}, {}, {}, {}
+        attn_words, h_words, grouped, attn_mx, h_mx = {}, {}, {}, {}, {}
+        attn_wo, x_mid, sum_sq, mean_sq, inv_rms, scaled, h = {}, {}, {}, {}, {}, {}, {}
+        gate, up, silu_gate = {}, {}, {}
 
         def tiles_of(q):
             return slice(q * BLOCK, (q + 1) * BLOCK)
@@ -63,29 +69,29 @@ def tile_transformerblocktpu_pb_t_kernel(
             nc.sync.dma_start(out=x_in[q][:], in_=x_tiles[:, tiles_of(q), :])
 
         def load_weight(w):
-            raw = stage.tile([P, PACK, D], BF16)
+            raw = weights.tile([P, PACK, D], BF16)
             nc.sync.dma_start(out=raw[:], in_=w.rearrange("(p t) n -> p t n", t=PACK))
             return raw
 
         def regroup_weight(raw, copy):
-            grouped = stage.tile([P, D, PACK], BF16, align_bytes=64)
+            columns = weights.tile([P, D, PACK], BF16, align_bytes=64)
             copy(
-                out=grouped[:].rearrange("p (c i) t -> p c t i", i=4),
+                out=columns[:].rearrange("p (c i) t -> p c t i", i=4),
                 in_=raw[:].rearrange("p t (c i) -> p c t i", i=4),
             )
-            return grouped
+            return columns
 
-        def quantise_weight(grouped, label):
+        def quantise_weight(columns, label):
             codes = keep.tile([P, D], U32, name=label + "_codes", align_bytes=64)
             scales = keep.tile([P, D], U8, name=label + "_scales", align_bytes=64)
             nc.vector.quantize_mx(
-                out=codes[:].bitcast(FP8X4), scales=scales[:], in_=grouped[:].rearrange("p n t -> p (n t)")
+                out=codes[:].bitcast(FP8X4), scales=scales[:], in_=columns[:].rearrange("p n t -> p (n t)")
             )
             return codes, scales
 
-        def transpose(rows):
+        def transpose(rows, tiles=range(BLOCK)):
             words = word_banks.tile([P, BLOCK, HALVES, P], F32)
-            for b in range(BLOCK):
+            for b in tiles:
                 row_words = rows[:, b, :].bitcast(F32)
                 for u in range(HALVES):
                     nc.tensor.transpose(words[:, b, u, :], row_words[:, u : HALVES * P : HALVES], identity[:])
@@ -110,8 +116,8 @@ def tile_transformerblocktpu_pb_t_kernel(
                 scales=scales[:, filled, :].rearrange("p c r -> p (c r)"),
                 in_=rows[:, filled, :, :, :].rearrange("p c b r t -> p (c b r t)"),
             )
-            h_mx[step - 2] = codes[:, 0, :], scales[:, 0, :]
-            attn_mx[step + 2] = codes[:, 1, :], scales[:, 1, :]
+            h_mx[step - H_LAG] = codes[:, 0, :], scales[:, 0, :]
+            attn_mx[step + ATTN_LEAD] = codes[:, 1, :], scales[:, 1, :]
 
         def product(rows_mx, b, weight_mx):
             bank = product_banks.tile([P, D], F32)
@@ -131,7 +137,7 @@ def tile_transformerblocktpu_pb_t_kernel(
             attn_words[q] = transpose(attn_in[q])
 
         def regroup_attn(q):
-            regroup(q - 2, 1, attn_words[q])
+            regroup(q - ATTN_LEAD, 1, attn_words[q])
 
         def multiply_by_w_o(q, b):
             attn_wo[q, b] = product(attn_mx[q], b, wo_mx)
@@ -164,29 +170,37 @@ def tile_transformerblocktpu_pb_t_kernel(
             nc.gpsimd.tensor_tensor(out=inv_rms[q][:], in0=mean_sq[q][:], in1=minus_half[:], op=ALU.pow)
 
         def scale_by_gain(q):
-            if q < FIRST_SHARED:
-                return
-            scaled[q] = work.tile([P, SHARED], F32, name="scaled")
-            nc.gpsimd.tensor_tensor(
-                out=scaled[q][:], in0=x_mid[q][:, 0, :SHARED], in1=gain[:, :SHARED], op=ALU.mult
-            )
+            if q >= FIRST_SHARED:
+                scaled[q] = work.tile([P, GAIN_ON_GPSIMD], F32, name="scaled")
+                nc.gpsimd.tensor_tensor(
+                    out=scaled[q][:],
+                    in0=x_mid[q][:, 0, :GAIN_ON_GPSIMD],
+                    in1=gain[:, :GAIN_ON_GPSIMD],
+                    op=ALU.mult,
+                )
 
         def scale_by_inv_rms(q):
             h[q] = work.tile([P, BLOCK, D], BF16, name="h")
-            if q < FIRST_SHARED:
-                return
-            nc.scalar.activation(
-                out=h[q][:, 0, :SCALAR], in_=scaled[q][:, :SCALAR], func=ACT.Copy, scale=inv_rms[q][:, 0:1]
-            )
+            if q >= FIRST_SHARED:
+                nc.scalar.activation(
+                    out=h[q][:, 0, :INV_ON_SCALAR],
+                    in_=scaled[q][:, :INV_ON_SCALAR],
+                    func=ACT.Copy,
+                    scale=inv_rms[q][:, 0:1],
+                )
 
         def normalise(q, b):
-            first = SHARED if b == 0 and q >= FIRST_SHARED else 0
-            if first > 0 and SCALAR < SHARED:
+            first = 0
+            if q >= FIRST_SHARED and b == 0:
                 nc.vector.tensor_scalar(
-                    out=h[q][:, 0, SCALAR:SHARED], in0=scaled[q][:, SCALAR:], scalar1=inv_rms[q][:, 0:1], scalar2=0.0, op0=ALU.mult, op1=ALU.add
+                    out=h[q][:, 0, INV_ON_SCALAR:GAIN_ON_GPSIMD],
+                    in0=scaled[q][:, INV_ON_SCALAR:],
+                    scalar1=inv_rms[q][:, 0:1],
+                    scalar2=0.0,
+                    op0=ALU.mult,
+                    op1=ALU.add,
                 )
-            if first == D:
-                return
+                first = GAIN_ON_GPSIMD
             nc.vector.scalar_tensor_tensor(
                 out=h[q][:, b, first:],
                 in0=x_mid[q][:, b, first:],
@@ -200,7 +214,7 @@ def tile_transformerblocktpu_pb_t_kernel(
             h_words[q] = transpose(h[q])
 
         def regroup_h(q):
-            regroup(q + 2, 0, h_words[q])
+            regroup(q + H_LAG, 0, h_words[q])
 
         def multiply_by_w_gate(q, b):
             gate[q, b] = product(h_mx[q], b, wg_mx)
@@ -216,11 +230,6 @@ def tile_transformerblocktpu_pb_t_kernel(
             g = per_tile.tile([P, D], F32)
             nc.vector.tensor_tensor(out=g[:], in0=up[q, b][:], in1=silu_gate[q, b][:], op=ALU.mult)
             nc.sync.dma_start(out=g_tiles[:, q * BLOCK + b, :], in_=g[:])
-
-        def keep_warm(products):
-            bank = product_banks.tile([P, D], F32)
-            for i in range(products):
-                nc.tensor.matmul(out=bank[:], lhsT=zeros[:, :P], rhs=zeros[:], start=True, stop=True)
 
         identity = keep.tile([P, P], F32)
         make_identity(nc, identity[:])
@@ -245,30 +254,18 @@ def tile_transformerblocktpu_pb_t_kernel(
         load_attn(2)
         wg_raw = load_weight(w_gate)
         load_x(1)
-        load_attn(3)
-        load_x(2)
-        load_attn(4)
-        load_x(3)
-        load_attn(5)
-        load_x(4)
-        load_attn(6)
-        load_x(5)
-        load_attn(7)
-        load_x(6)
-        load_attn(8)
-        load_x(7)
-        load_attn(9)
-        load_x(8)
+        for q in range(3, 10):
+            load_attn(q)
+            load_x(q - 1)
 
-        def at(q, stage_of_block, *tile):
-            if 0 <= q < BLOCKS:
-                stage_of_block(q, *tile)
+        warm_bank = product_banks.tile([P, D], F32, tag="bank")
+        for i in range(WARM_PRODUCTS):
+            nc.tensor.matmul(out=warm_bank[:], lhsT=zeros[:, :P], rhs=zeros[:], start=True, stop=True)
 
-        keep_warm(5)
         transpose_attn(0)
-        wo_grouped = regroup_weight(wo_raw, nc.vector.tensor_copy)
+        wo_columns = regroup_weight(wo_raw, nc.vector.tensor_copy)
         regroup_attn(0)
-        wo_mx = quantise_weight(wo_grouped, "wo")
+        wo_mx = quantise_weight(wo_columns, "wo")
         quantise(-2)
         transpose_attn(1)
         multiply_by_w_o(0, 0)
@@ -276,11 +273,11 @@ def tile_transformerblocktpu_pb_t_kernel(
         gain_bank = product_banks.tile([P, D], F32, tag="bank")
         nc.tensor.matmul(out=gain_bank[:], lhsT=ones[:], rhs=gain_row[:], start=True, stop=True)
         regroup_attn(1)
-        wu_grouped = regroup_weight(wu_raw, nc.scalar.copy)
+        wu_columns = regroup_weight(wu_raw, nc.scalar.copy)
         add_residual(0, 0)
         add_residual(0, 1)
         quantise(-1)
-        wg_grouped = regroup_weight(wg_raw, nc.vector.tensor_copy)
+        wg_columns = regroup_weight(wg_raw, nc.vector.tensor_copy)
         transpose_attn(2)
         multiply_by_w_o(1, 0)
         multiply_by_w_o(1, 1)
@@ -289,12 +286,13 @@ def tile_transformerblocktpu_pb_t_kernel(
         regroup_attn(2)
         gain = keep.tile([P, D], F32)
         nc.scalar.copy(out=gain[:], in_=gain_bank[:])
+
         add_residual(1, 0)
         mean_squares(0)
         invert_rms(0)
         add_residual(1, 1)
         quantise(0)
-        wg_mx = quantise_weight(wg_grouped, "wg")
+        wg_mx = quantise_weight(wg_columns, "wg")
         transpose_attn(3)
         multiply_by_w_o(2, 0)
         multiply_by_w_o(2, 1)
@@ -304,12 +302,13 @@ def tile_transformerblocktpu_pb_t_kernel(
         regroup_attn(3)
         normalise(0, 0)
         normalise(0, 1)
+
         transpose_attn(4)
         transpose_h(0)
         mean_squares(1)
         invert_rms(1)
         quantise(1)
-        wu_mx = quantise_weight(wu_grouped, "wu")
+        wu_mx = quantise_weight(wu_columns, "wu")
         regroup_attn(4)
         regroup_h(0)
         add_residual(2, 0)
@@ -321,6 +320,7 @@ def tile_transformerblocktpu_pb_t_kernel(
         sum_squares(2, 1)
         normalise(1, 0)
         normalise(1, 1)
+
         transpose_attn(5)
         transpose_h(1)
         mean_squares(2)
@@ -341,31 +341,71 @@ def tile_transformerblocktpu_pb_t_kernel(
         sum_squares(3, 1)
         normalise(2, 0)
         normalise(2, 1)
-        for step in range(4, BLOCKS + 4):
-            at(step + 6, load_attn)
-            at(step + 5, load_x)
-            at(step + 2, transpose_attn)
-            at(step - 2, transpose_h)
+
+        def at(stage, q):
+            if 0 <= q < BLOCKS:
+                stage(q)
+
+        def at_tiles(stage, q):
+            if 0 <= q < BLOCKS:
+                for b in range(BLOCK):
+                    stage(q, b)
+
+        for step in range(G_LAG, BLOCKS + 1):
+            at(load_attn, step + 6)
+            at(load_x, step + 5)
+            at(transpose_attn, step + ATTN_LEAD)
+            at(transpose_h, step - H_LAG)
             quantise(step - 1)
-            at(step - 1, mean_squares)
-            at(step - 1, invert_rms)
-            at(step - 4, apply_silu, 0)
-            at(step - 4, apply_silu, 1)
-            at(step + 2, regroup_attn)
-            at(step - 2, regroup_h)
-            at(step - 3, multiply_by_w_gate, 0)
-            at(step - 3, multiply_by_w_gate, 1)
-            at(step, add_residual, 0)
-            at(step, add_residual, 1)
-            at(step + 1, multiply_by_w_o, 0)
-            at(step + 1, multiply_by_w_o, 1)
-            at(step - 4, multiply_gate_and_up, 0)
-            at(step - 4, multiply_gate_and_up, 1)
-            at(step - 3, multiply_by_w_up, 0)
-            at(step - 3, multiply_by_w_up, 1)
-            at(step - 1, scale_by_inv_rms)
-            at(step, sum_squares, 0)
-            at(step, sum_squares, 1)
-            at(step, scale_by_gain)
-            at(step - 1, normalise, 0)
-            at(step - 1, normalise, 1)
+            at(mean_squares, step - 1)
+            at(invert_rms, step - 1)
+            at_tiles(apply_silu, step - G_LAG)
+            at(regroup_attn, step + ATTN_LEAD)
+            at(regroup_h, step - H_LAG)
+            at_tiles(multiply_by_w_gate, step - 3)
+            at_tiles(add_residual, step)
+            at_tiles(multiply_by_w_o, step + 1)
+            at_tiles(multiply_gate_and_up, step - G_LAG)
+            at_tiles(multiply_by_w_up, step - 3)
+            at(scale_by_inv_rms, step - 1)
+            at_tiles(sum_squares, step)
+            at(scale_by_gain, step)
+            at_tiles(normalise, step - 1)
+
+        last = BLOCKS - 1
+        last_rows = work.tile([P, BLOCK, P, PACK], BF16, align_bytes=64)
+        last_codes = work.tile([P, BLOCK * P], U32, align_bytes=64)
+        last_scales = work.tile([P, BLOCK * P], U8, align_bytes=64)
+        h_mx[last] = last_codes, last_scales
+
+        def regroup_last(b, words):
+            nc.scalar.copy(
+                out=last_rows[:, b, :, :].bitcast(F32), in_=words[:, b, :, :].rearrange("p u r -> p r u")
+            )
+
+        def quantise_last(b):
+            tokens = slice(b * P, (b + 1) * P)
+            nc.vector.quantize_mx(
+                out=last_codes[:, tokens].bitcast(FP8X4),
+                scales=last_scales[:, tokens],
+                in_=last_rows[:, b, :, :].rearrange("p r t -> p (r t)"),
+            )
+
+        first_words = transpose(h[last], [0])
+        quantise(BLOCKS)
+        at_tiles(apply_silu, last - 2)
+        regroup_last(0, first_words)
+        second_words = transpose(h[last], [1])
+        regroup_last(1, second_words)
+        at_tiles(multiply_by_w_gate, last - 1)
+        at_tiles(multiply_gate_and_up, last - 2)
+        at_tiles(multiply_by_w_up, last - 1)
+        quantise_last(0)
+        quantise_last(1)
+        at_tiles(apply_silu, last - 1)
+        for b in range(BLOCK):
+            multiply_gate_and_up(last - 1, b)
+            multiply_by_w_gate(last, b)
+            multiply_by_w_up(last, b)
+        at_tiles(apply_silu, last)
+        at_tiles(multiply_gate_and_up, last)

from contextlib import ExitStack

import concourse.mybir as mybir
from concourse.masks import make_identity

F32 = mybir.dt.float32
BF16 = mybir.dt.bfloat16
U32 = mybir.dt.uint32
U8 = mybir.dt.uint8
FP8X4 = mybir.dt.float8_e4m3fn_x4
ALU = mybir.AluOpType
ACT = mybir.ActivationFunctionType

P = 128
PACK = 4
HALVES = 2
D = 512
TOKENS = 4096
BLOCK = 2
BLOCKS = TOKENS // (P * BLOCK)
EPS = 1e-6

ATTN_LEAD = 2
H_LAG = 2
G_LAG = 4

GAIN_ON_GPSIMD = 384
INV_ON_SCALAR = 256
FIRST_SHARED = G_LAG
WARM_PRODUCTS = 5

FLOPS = 3 * 2 * TOKENS * D * D


def tile_transformerblocktpu_pb_t_kernel(
    tc, attn, x, w_o, rms2_scale, w_gate, w_up, out_0, out_1
):
    nc = tc.nc
    attn_tiles = attn.flatten_outer_dims().rearrange("(p j) k -> p j k", p=P)
    x_tiles = x.flatten_outer_dims().rearrange("(p j) k -> p j k", p=P)
    x_mid_tiles = out_0.flatten_outer_dims().rearrange("(p j) k -> p j k", p=P)
    g_tiles = out_1.flatten_outer_dims().rearrange("(p j) k -> p j k", p=P)

    with ExitStack() as pools:
        pools.enter_context(tc.manual_schedule())
        keep = pools.enter_context(tc.tile_pool(name="keep", bufs=1))
        weights = pools.enter_context(tc.tile_pool(name="weights", bufs=3))
        loads = pools.enter_context(tc.tile_pool(name="loads", bufs=BLOCKS))
        results = pools.enter_context(tc.tile_pool(name="results", bufs=4))
        work = pools.enter_context(tc.tile_pool(name="work", bufs=3))
        per_tile = pools.enter_context(tc.tile_pool(name="per_tile", bufs=3 * BLOCK))
        word_banks = pools.enter_context(tc.psum_pool(name="word_banks", bufs=2))
        product_banks = pools.enter_context(tc.psum_pool(name="product_banks", bufs=3 * BLOCK))

        attn_in, x_in = {}, {}
        attn_words, h_words, grouped, attn_mx, h_mx = {}, {}, {}, {}, {}
        attn_wo, x_mid, sum_sq, mean_sq, inv_rms, scaled, h = {}, {}, {}, {}, {}, {}, {}
        gate, up, silu_gate = {}, {}, {}

        def tiles_of(q):
            return slice(q * BLOCK, (q + 1) * BLOCK)

        def load_attn(q):
            attn_in[q] = loads.tile([P, BLOCK, D], BF16, name="attn_in")
            nc.sync.dma_start(out=attn_in[q][:], in_=attn_tiles[:, tiles_of(q), :])

        def load_x(q):
            x_in[q] = loads.tile([P, BLOCK, D], BF16, name="x_in")
            nc.sync.dma_start(out=x_in[q][:], in_=x_tiles[:, tiles_of(q), :])

        def load_weight(w):
            raw = weights.tile([P, PACK, D], BF16)
            nc.sync.dma_start(out=raw[:], in_=w.rearrange("(p t) n -> p t n", t=PACK))
            return raw

        def regroup_weight(raw, copy):
            columns = weights.tile([P, D, PACK], BF16, align_bytes=64)
            copy(
                out=columns[:].rearrange("p (c i) t -> p c t i", i=4),
                in_=raw[:].rearrange("p t (c i) -> p c t i", i=4),
            )
            return columns

        def quantise_weight(columns, label):
            codes = keep.tile([P, D], U32, name=label + "_codes", align_bytes=64)
            scales = keep.tile([P, D], U8, name=label + "_scales", align_bytes=64)
            nc.vector.quantize_mx(
                out=codes[:].bitcast(FP8X4), scales=scales[:], in_=columns[:].rearrange("p n t -> p (n t)")
            )
            return codes, scales

        def transpose(rows, tiles=range(BLOCK)):
            words = word_banks.tile([P, BLOCK, HALVES, P], F32)
            for b in tiles:
                row_words = rows[:, b, :].bitcast(F32)
                for u in range(HALVES):
                    nc.tensor.transpose(words[:, b, u, :], row_words[:, u : HALVES * P : HALVES], identity[:])
            return words

        def regroup(step, place, words):
            if step not in grouped:
                grouped[step] = work.tile([P, 2, BLOCK, P, PACK], BF16, name="grouped", align_bytes=64), []
            rows, places = grouped[step]
            places.append(place)
            nc.scalar.copy(out=rows[:, place, :, :, :].bitcast(F32), in_=words[:].rearrange("p b u r -> p b r u"))

        def quantise(step):
            if step not in grouped:
                return
            rows, places = grouped[step]
            codes = work.tile([P, 2, BLOCK * P], U32, name="codes", align_bytes=64)
            scales = work.tile([P, 2, BLOCK * P], U8, name="scales", align_bytes=64)
            filled = slice(min(places), max(places) + 1)
            nc.vector.quantize_mx(
                out=codes[:, filled, :].rearrange("p c r -> p (c r)").bitcast(FP8X4),
                scales=scales[:, filled, :].rearrange("p c r -> p (c r)"),
                in_=rows[:, filled, :, :, :].rearrange("p c b r t -> p (c b r t)"),
            )
            h_mx[step - H_LAG] = codes[:, 0, :], scales[:, 0, :]
            attn_mx[step + ATTN_LEAD] = codes[:, 1, :], scales[:, 1, :]

        def product(rows_mx, b, weight_mx):
            bank = product_banks.tile([P, D], F32)
            tokens = slice(b * P, (b + 1) * P)
            nc.tensor.matmul_mx(
                out=bank[:],
                lhsT=rows_mx[0][:, tokens].bitcast(FP8X4),
                lhsT_scale=rows_mx[1][:, tokens],
                rhs=weight_mx[0][:].bitcast(FP8X4),
                rhs_scale=weight_mx[1][:],
                start=True,
                stop=True,
            )
            return bank

        def transpose_attn(q):
            attn_words[q] = transpose(attn_in[q])

        def regroup_attn(q):
            regroup(q - ATTN_LEAD, 1, attn_words[q])

        def multiply_by_w_o(q, b):
            attn_wo[q, b] = product(attn_mx[q], b, wo_mx)

        def add_residual(q, b):
            if b == 0:
                x_mid[q] = results.tile([P, BLOCK, D], F32, name="x_mid")
            nc.vector.tensor_tensor(
                out=x_mid[q][:, b, :], in0=attn_wo[q, b][:], in1=x_in[q][:, b, :], op=ALU.add
            )
            if b == BLOCK - 1:
                nc.sync.dma_start(out=x_mid_tiles[:, tiles_of(q), :], in_=x_mid[q][:])

        def sum_squares(q, b):
            if b == 0:
                sum_sq[q] = work.tile([P, BLOCK], F32, name="sum_sq")
            squares = per_tile.tile([P, D], BF16)
            nc.scalar.activation(
                out=squares[:], in_=x_mid[q][:, b, :], func=ACT.Square, accum_out=sum_sq[q][:, b : b + 1]
            )

        def mean_squares(q):
            mean_sq[q] = work.tile([P, BLOCK], F32, name="mean_sq")
            nc.vector.tensor_scalar(
                out=mean_sq[q][:], in0=sum_sq[q][:], scalar1=1.0 / D, scalar2=EPS, op0=ALU.mult, op1=ALU.add
            )

        def invert_rms(q):
            inv_rms[q] = work.tile([P, BLOCK], F32, name="inv_rms")
            nc.gpsimd.tensor_tensor(out=inv_rms[q][:], in0=mean_sq[q][:], in1=minus_half[:], op=ALU.pow)

        def scale_by_gain(q):
            if q >= FIRST_SHARED:
                scaled[q] = work.tile([P, GAIN_ON_GPSIMD], F32, name="scaled")
                nc.gpsimd.tensor_tensor(
                    out=scaled[q][:],
                    in0=x_mid[q][:, 0, :GAIN_ON_GPSIMD],
                    in1=gain[:, :GAIN_ON_GPSIMD],
                    op=ALU.mult,
                )

        def scale_by_inv_rms(q):
            h[q] = work.tile([P, BLOCK, D], BF16, name="h")
            if q >= FIRST_SHARED:
                nc.scalar.activation(
                    out=h[q][:, 0, :INV_ON_SCALAR],
                    in_=scaled[q][:, :INV_ON_SCALAR],
                    func=ACT.Copy,
                    scale=inv_rms[q][:, 0:1],
                )

        def normalise(q, b):
            first = 0
            if q >= FIRST_SHARED and b == 0:
                nc.vector.tensor_scalar(
                    out=h[q][:, 0, INV_ON_SCALAR:GAIN_ON_GPSIMD],
                    in0=scaled[q][:, INV_ON_SCALAR:],
                    scalar1=inv_rms[q][:, 0:1],
                    scalar2=0.0,
                    op0=ALU.mult,
                    op1=ALU.add,
                )
                first = GAIN_ON_GPSIMD
            nc.vector.scalar_tensor_tensor(
                out=h[q][:, b, first:],
                in0=x_mid[q][:, b, first:],
                scalar=inv_rms[q][:, b : b + 1],
                in1=gain[:, first:],
                op0=ALU.mult,
                op1=ALU.mult,
            )

        def transpose_h(q):
            h_words[q] = transpose(h[q])

        def regroup_h(q):
            regroup(q + H_LAG, 0, h_words[q])

        def multiply_by_w_gate(q, b):
            gate[q, b] = product(h_mx[q], b, wg_mx)

        def multiply_by_w_up(q, b):
            up[q, b] = product(h_mx[q], b, wu_mx)

        def apply_silu(q, b):
            silu_gate[q, b] = per_tile.tile([P, D], F32, name="silu_gate")
            nc.scalar.activation(out=silu_gate[q, b][:], in_=gate[q, b][:], func=ACT.Silu)

        def multiply_gate_and_up(q, b):
            g = per_tile.tile([P, D], F32)
            nc.vector.tensor_tensor(out=g[:], in0=up[q, b][:], in1=silu_gate[q, b][:], op=ALU.mult)
            nc.sync.dma_start(out=g_tiles[:, q * BLOCK + b, :], in_=g[:])

        identity = keep.tile([P, P], F32)
        make_identity(nc, identity[:])
        zeros = keep.tile([P, D], BF16)
        nc.vector.memset(zeros[:], 0.0)
        gain_row = keep.tile([P, D], BF16)
        nc.vector.memset(gain_row[:], 0.0)
        ones = keep.tile([P, P], BF16)
        nc.vector.memset(ones[:], 1.0)
        minus_half = keep.tile([P, BLOCK], F32)
        nc.vector.memset(minus_half[:], -0.5)

        table_warmer = keep.tile([P, BLOCK], F32)
        nc.scalar.activation(out=table_warmer[:], in_=minus_half[:], func=ACT.Silu)

        wo_raw = load_weight(w_o)
        load_attn(0)
        load_attn(1)
        nc.sync.dma_start(out=gain_row[0:1, :], in_=rms2_scale.rearrange("(o n) -> o n", o=1))
        load_x(0)
        wu_raw = load_weight(w_up)
        load_attn(2)
        wg_raw = load_weight(w_gate)
        load_x(1)
        for q in range(3, 10):
            load_attn(q)
            load_x(q - 1)

        warm_bank = product_banks.tile([P, D], F32, tag="bank")
        for i in range(WARM_PRODUCTS):
            nc.tensor.matmul(out=warm_bank[:], lhsT=zeros[:, :P], rhs=zeros[:], start=True, stop=True)

        transpose_attn(0)
        wo_columns = regroup_weight(wo_raw, nc.vector.tensor_copy)
        regroup_attn(0)
        wo_mx = quantise_weight(wo_columns, "wo")
        quantise(-2)
        transpose_attn(1)
        multiply_by_w_o(0, 0)
        multiply_by_w_o(0, 1)
        gain_bank = product_banks.tile([P, D], F32, tag="bank")
        nc.tensor.matmul(out=gain_bank[:], lhsT=ones[:], rhs=gain_row[:], start=True, stop=True)
        regroup_attn(1)
        wu_columns = regroup_weight(wu_raw, nc.scalar.copy)
        add_residual(0, 0)
        add_residual(0, 1)
        quantise(-1)
        wg_columns = regroup_weight(wg_raw, nc.vector.tensor_copy)
        transpose_attn(2)
        multiply_by_w_o(1, 0)
        multiply_by_w_o(1, 1)
        sum_squares(0, 0)
        sum_squares(0, 1)
        regroup_attn(2)
        gain = keep.tile([P, D], F32)
        nc.scalar.copy(out=gain[:], in_=gain_bank[:])

        add_residual(1, 0)
        mean_squares(0)
        invert_rms(0)
        add_residual(1, 1)
        quantise(0)
        wg_mx = quantise_weight(wg_columns, "wg")
        transpose_attn(3)
        multiply_by_w_o(2, 0)
        multiply_by_w_o(2, 1)
        scale_by_inv_rms(0)
        sum_squares(1, 0)
        sum_squares(1, 1)
        regroup_attn(3)
        normalise(0, 0)
        normalise(0, 1)

        transpose_attn(4)
        transpose_h(0)
        mean_squares(1)
        invert_rms(1)
        quantise(1)
        wu_mx = quantise_weight(wu_columns, "wu")
        regroup_attn(4)
        regroup_h(0)
        add_residual(2, 0)
        add_residual(2, 1)
        multiply_by_w_o(3, 0)
        multiply_by_w_o(3, 1)
        scale_by_inv_rms(1)
        sum_squares(2, 0)
        sum_squares(2, 1)
        normalise(1, 0)
        normalise(1, 1)

        transpose_attn(5)
        transpose_h(1)
        mean_squares(2)
        invert_rms(2)
        quantise(2)
        regroup_attn(5)
        regroup_h(1)
        multiply_by_w_gate(0, 0)
        multiply_by_w_gate(0, 1)
        add_residual(3, 0)
        add_residual(3, 1)
        multiply_by_w_o(4, 0)
        multiply_by_w_o(4, 1)
        multiply_by_w_up(0, 0)
        multiply_by_w_up(0, 1)
        scale_by_inv_rms(2)
        sum_squares(3, 0)
        sum_squares(3, 1)
        normalise(2, 0)
        normalise(2, 1)

        def at(stage, q):
            if 0 <= q < BLOCKS:
                stage(q)

        def at_tiles(stage, q):
            if 0 <= q < BLOCKS:
                for b in range(BLOCK):
                    stage(q, b)

        for step in range(G_LAG, BLOCKS + 1):
            at(load_attn, step + 6)
            at(load_x, step + 5)
            at(transpose_attn, step + ATTN_LEAD)
            at(transpose_h, step - H_LAG)
            quantise(step - 1)
            at(mean_squares, step - 1)
            at(invert_rms, step - 1)
            at_tiles(apply_silu, step - G_LAG)
            at(regroup_attn, step + ATTN_LEAD)
            at(regroup_h, step - H_LAG)
            at_tiles(multiply_by_w_gate, step - 3)
            at_tiles(add_residual, step)
            at_tiles(multiply_by_w_o, step + 1)
            at_tiles(multiply_gate_and_up, step - G_LAG)
            at_tiles(multiply_by_w_up, step - 3)
            at(scale_by_inv_rms, step - 1)
            at_tiles(sum_squares, step)
            at(scale_by_gain, step)
            at_tiles(normalise, step - 1)

        last = BLOCKS - 1
        last_rows = work.tile([P, BLOCK, P, PACK], BF16, align_bytes=64)
        last_codes = work.tile([P, BLOCK * P], U32, align_bytes=64)
        last_scales = work.tile([P, BLOCK * P], U8, align_bytes=64)
        h_mx[last] = last_codes, last_scales

        def regroup_last(b, words):
            nc.scalar.copy(
                out=last_rows[:, b, :, :].bitcast(F32), in_=words[:, b, :, :].rearrange("p u r -> p r u")
            )

        def quantise_last(b):
            tokens = slice(b * P, (b + 1) * P)
            nc.vector.quantize_mx(
                out=last_codes[:, tokens].bitcast(FP8X4),
                scales=last_scales[:, tokens],
                in_=last_rows[:, b, :, :].rearrange("p r t -> p (r t)"),
            )

        first_words = transpose(h[last], [0])
        quantise(BLOCKS)
        at_tiles(apply_silu, last - 2)
        regroup_last(0, first_words)
        second_words = transpose(h[last], [1])
        regroup_last(1, second_words)
        at_tiles(multiply_by_w_gate, last - 1)
        at_tiles(multiply_gate_and_up, last - 2)
        at_tiles(multiply_by_w_up, last - 1)
        quantise_last(0)
        quantise_last(1)
        at_tiles(apply_silu, last - 1)
        for b in range(BLOCK):
            multiply_gate_and_up(last - 1, b)
            multiply_by_w_gate(last, b)
            multiply_by_w_up(last, b)
        at_tiles(apply_silu, last)
        at_tiles(multiply_gate_and_up, last)
